import numpy as np
import ml_dtypes


def mxq(x, axis, fmt="e4m3"):
    dtype, down = {"e4m3": (ml_dtypes.float8_e4m3fn, 7), "e5m2": (ml_dtypes.float8_e5m2, 14)}[fmt]
    v = np.moveaxis(np.asarray(x, np.float32).astype(ml_dtypes.bfloat16).astype(np.float64), axis, -1)
    blocks = v.reshape(v.shape[:-1] + (-1, 32))
    amax = np.abs(blocks).max(-1, keepdims=True)
    byte = np.maximum(np.where(amax > 0, np.frexp(amax)[1] - 1 + 127, 0) - down, 1)
    scale = np.exp2(byte - 127.0)
    codes = (blocks / scale).astype(np.float32).astype(dtype).astype(np.float64)
    return np.moveaxis((codes * scale).reshape(v.shape), -1, axis)


WIDE = False


def mx_kscale(k):
    if not WIDE:
        return np.ones(k)
    levels = np.array([10, -10, 5, -5, 0])
    a = np.random.permutation(np.resize(levels, k // 512 * 4)).reshape(k // 512, 4)
    idx = np.arange(k)
    return np.exp2(a[idx // 512, idx % 128 // 32])


BF16 = ml_dtypes.bfloat16


def bf(x):
    return np.asarray(x, np.float32).astype(BF16)


def f64(x):
    return np.asarray(x).astype(np.float64)


E2M1 = np.array([0.0, 0.5, 1.0, 1.5, 2.0, 3.0, 4.0, 6.0, -0.0, -0.5, -1.0, -1.5, -2.0, -3.0, -4.0, -6.0])


def pack_weight(w, fmt):
    k, n = w.shape
    w = f64(bf(w)).reshape(k // 32, 32, n)
    amax = np.abs(w).max(1)
    if fmt == "e4m3":
        byte = np.frexp(amax)[1] - 1 + 127 - 7
    else:
        mant, ex = np.frexp(amax / 6.0)
        byte = np.where(mant > 0.5, ex, ex - 1) + 127
    byte = np.clip(np.where(amax > 0, byte, 1), 1, 254)
    scaled = (w * np.exp2(127.0 - byte)[:, None, :]).reshape(k, n).astype(np.float32)
    by_word = np.ascontiguousarray(scaled.reshape(k // 512, 128, 4, n).transpose(0, 1, 3, 2))
    if fmt == "e4m3":
        words = by_word.astype(ml_dtypes.float8_e4m3fn).view(np.uint8)
    else:
        c = by_word.astype(ml_dtypes.float4_e2m1fn).view(np.uint8) & 0xF
        words = c[..., 0::2] | (c[..., 1::2] << 4)
    return np.ascontiguousarray(words), np.ascontiguousarray(byte.astype(np.uint8).reshape(k // 512, 16, n))


def unpack_weight(words, scales, fmt):
    g, p, n, _ = words.shape
    if fmt == "e4m3":
        vals = np.ascontiguousarray(words).view(ml_dtypes.float8_e4m3fn).astype(np.float64)
    else:
        nib = np.empty((g, p, n, 4), np.uint8)
        nib[..., 0::2] = words & 0xF
        nib[..., 1::2] = words >> 4
        vals = E2M1[nib]
    vals = vals * np.repeat(np.exp2(scales.astype(np.float64) - 127.0), 8, axis=1)[..., None]
    return vals.transpose(0, 1, 3, 2).reshape(g * 512, n)

def pack4(w):
    words, scales = pack_weight(w, "e2m1")
    return words.reshape(words.shape[0], 128, -1), scales


def unpack4(words, scales):
    return unpack_weight(words.reshape(words.shape[0], 128, -1, 2), scales, "e2m1")


B, D, H, K = 5120, 1024, 1024, 128
EPS_B = 1e-8


def silu(v):
    return v / (1.0 + np.exp(-v))


def softplus(v):
    return np.maximum(v, 0.0) + np.log(1.0 + np.exp(-np.abs(v)))


def setup_inputs():
    s = mx_kscale(H)
    h_act = bf(silu(np.random.standard_normal((B, H))) * s)
    W3_words, W3_scales = pack4(np.random.standard_normal((H, K)) * 3.0 / np.sqrt(H) / s[:, None])
    b3 = bf(0.5 * np.random.standard_normal(K))
    return {"h_act": h_act,
            "W3_words": W3_words,
            "W3_scales": W3_scales,
            "b3": b3}


def reference(h_act, W3_words, W3_scales, b3):
    logits = (mxq(f64(h_act), 1, "e4m3") @ unpack4(W3_words, W3_scales)) + f64(b3)
    evidence = softplus(logits)
    alpha = evidence + 1.0
    S = alpha.sum(-1, keepdims=True)
    expected_prob = alpha / S
    vacuity = float(K) / S[:, 0]
    belief = evidence / S
    full = np.zeros(belief.shape[0])
    for i in range(K):
        bi = belief[:, i:i + 1]
        full = full + ((1.0 - np.abs(bi - belief) / (bi + belief + EPS_B)) * bi * belief).sum(-1)
    dissonance = 0.5 * (full - (belief * belief).sum(-1))
    return (alpha, evidence, expected_prob, vacuity, dissonance)

@@ -1,0 +1,282 @@
+from contextlib import ExitStack
+
+import concourse.mybir as mybir
+from concourse.masks import make_identity
+
+F32 = mybir.dt.float32
+BF16 = mybir.dt.bfloat16
+I32 = mybir.dt.int32
+U32 = mybir.dt.uint32
+U8 = mybir.dt.uint8
+FP8X4 = mybir.dt.float8_e4m3fn_x4
+FP4X4 = mybir.dt.float4_e2m1fn_x4
+ALU = mybir.AluOpType
+ACT = mybir.ActivationFunctionType
+AXIS_X = mybir.AxisListType.X
+
+P = 128
+ROWS = 5120
+K = 1024
+CLASSES = 128
+CLASS_BITS = 7
+EPS = 1e-8
+PASSES = K // 512
+TILES = ROWS // P
+GROUP = 4
+GROUPS = TILES // GROUP
+PAIRS = CLASSES * (CLASSES - 1) // 2
+
+FLOPS = 2 * ROWS * K * CLASSES
+
+
+def compare_exchange_stage(nc, src, dst, width, dist):
+    directions = 2 if width < CLASSES else 1
+    pattern = "p (a d b s j) g -> p a d b s (j g)"
+    sizes = dict(a=CLASSES // (width * directions), d=directions, b=width // (2 * dist), s=2, j=dist)
+    src_view = src.rearrange(pattern, **sizes)
+    dst_view = dst.rearrange(pattern, **sizes)
+    for d in range(directions):
+        low_op, high_op = (ALU.min, ALU.max) if d == 0 else (ALU.max, ALU.min)
+        low = src_view[:, :, d, :, 0, :]
+        high = src_view[:, :, d, :, 1, :]
+        nc.vector.tensor_tensor(out=dst_view[:, :, d, :, 0, :], in0=low, in1=high, op=low_op)
+        nc.vector.tensor_tensor(out=dst_view[:, :, d, :, 1, :], in0=low, in1=high, op=high_op)
+
+
+def tile_evidentialhead_pb_kernel(tc, h_act, W3_words, W3_scales, b3, out_0, out_1, out_2, out_3, out_4):
+    nc = tc.nc
+    h_rows = h_act.rearrange("(p t) k -> p t k", t=TILES)
+    alpha_out = out_0.rearrange("(p t) c -> p t c", t=TILES)
+    evidence_out = out_1.rearrange("(p t) c -> p t c", t=TILES)
+    prob_out = out_2.rearrange("(p t) c -> p t c", t=TILES)
+    vacuity_out = out_3.rearrange("(p t) -> p t", t=TILES)
+    dissonance_out = out_4.rearrange("(p t) -> p t", t=TILES)
+
+    with ExitStack() as ctx:
+        ctx.enter_context(tc.manual_schedule())
+        const = ctx.enter_context(tc.tile_pool(name="const", bufs=1))
+        whole = ctx.enter_context(tc.tile_pool(name="whole", bufs=1))
+        h_pool = ctx.enter_context(tc.tile_pool(name="h", bufs=3))
+        mx_pool = ctx.enter_context(tc.tile_pool(name="mx", bufs=2))
+        out_pool = ctx.enter_context(tc.tile_pool(name="outs", bufs=2))
+        sort_pool = ctx.enter_context(tc.tile_pool(name="sort", bufs=1))
+        pair_pool = ctx.enter_context(tc.tile_pool(name="pair", bufs=2))
+        psum_t = ctx.enter_context(tc.psum_pool(name="psum_t", bufs=6))
+        psum_l = ctx.enter_context(tc.psum_pool(name="psum_l", bufs=2))
+
+        def group_tiles(g):
+            return slice(g * GROUP, (g + 1) * GROUP)
+
+        h_tiles = {}
+
+        def load_h(g):
+            h_sb = h_pool.tile([P, GROUP, K], BF16, name="h_sb")
+            nc.sync.dma_start(out=h_sb[:], in_=h_rows[:, group_tiles(g), :])
+            h_tiles[g] = h_sb
+
+        load_h(0)
+        w_scales = const.tile([P, PASSES, CLASSES], U8, align_bytes=64)
+        nc.vector.memset(w_scales[:].bitcast(I32), 0)
+        w_words = const.tile([P, PASSES, 2 * CLASSES], U8, align_bytes=64)
+        for c in range(PASSES):
+            nc.sync.dma_start(out=w_words[:, c, :].bitcast(I32), in_=W3_words[c].bitcast(I32))
+            for quadrant in range(4):
+                nc.sync.dma_start(
+                    out=w_scales[32 * quadrant : 32 * quadrant + 4, c, :].bitcast(I32),
+                    in_=W3_scales[c, 4 * quadrant : 4 * quadrant + 4, :].bitcast(I32),
+                )
+        bias_rows = const.tile([P, CLASSES], BF16)
+        nc.sync.dma_start(out=bias_rows[:], in_=b3.partition_broadcast(P))
+        load_h(1)
+
+        identity = const.tile([P, P], F32)
+        make_identity(nc, identity[:])
+        class_index = const.tile([P, CLASSES], I32)
+        nc.gpsimd.iota(class_index[:], pattern=[[1, CLASSES]], base=0, channel_multiplier=0)
+        classes_above = const.tile([P, CLASSES], F32)
+        nc.vector.tensor_scalar(
+            out=classes_above[:], in0=class_index[:], scalar1=-1.0, scalar2=float(CLASSES - 1), op0=ALU.mult, op1=ALU.add
+        )
+        one = const.tile([P, 1], F32)
+        nc.vector.memset(one[:], 1.0)
+        half_eps = const.tile([P, 1], F32)
+        nc.vector.memset(half_eps[:], EPS / 2)
+
+        logits = whole.tile([P, TILES, CLASSES], F32)
+        work = whole.tile([P, TILES, CLASSES], F32)
+        evidence = whole.tile([P, TILES, CLASSES], F32)
+        alpha_sum = whole.tile([P, TILES], F32)
+        inv_sum = whole.tile([P, TILES], F32)
+        vacuity = whole.tile([P, TILES], F32)
+        dissonance = whole.tile([P, TILES], F32)
+
+        mx_operands = {}
+
+        def quantise_group(g):
+            h_sb = h_tiles[g]
+            grouped = mx_pool.tile([P, GROUP, K], BF16, align_bytes=64)
+            for t in range(GROUP):
+                h_words = h_sb[:, t, :].bitcast(F32)
+                flipped = psum_t.tile([P, PASSES, 2, P], F32)
+                for c in range(PASSES):
+                    for u in range(2):
+                        nc.tensor.transpose(flipped[:, c, u, :], h_words[:, 256 * c + u : 256 * (c + 1) : 2], identity[:])
+                nc.scalar.copy(
+                    out=grouped[:, t, :].bitcast(F32).rearrange("p (c r u) -> p c r u", c=PASSES, u=2),
+                    in_=flipped[:].rearrange("p c u r -> p c r u"),
+                )
+            codes = mx_pool.tile([P, GROUP, PASSES * P], U32, align_bytes=64)
+            scales = mx_pool.tile([P, GROUP, PASSES * P], U8, align_bytes=64)
+            nc.vector.quantize_mx(
+                out=codes[:].rearrange("p t w -> p (t w)").bitcast(FP8X4),
+                scales=scales[:].rearrange("p t w -> p (t w)"),
+                in_=grouped[:].rearrange("p t k -> p (t k)"),
+            )
+            mx_operands[g] = (codes, scales)
+
+        def logits_group(g):
+            codes, scales = mx_operands[g]
+            acc = psum_l.tile([P, GROUP, CLASSES], F32)
+            for t in range(GROUP):
+                for c in range(PASSES):
+                    rows = slice(c * P, (c + 1) * P)
+                    nc.tensor.matmul_mx(
+                        out=acc[:, t, :],
+                        lhsT=codes[:, t, rows].bitcast(FP8X4),
+                        lhsT_scale=scales[:, t, rows],
+                        rhs=w_words[:, c, :].bitcast(FP4X4),
+                        rhs_scale=w_scales[:, c, :],
+                        start=(c == 0),
+                        stop=(c == PASSES - 1),
+                    )
+            tiles = group_tiles(g)
+            nc.vector.tensor_tensor(
+                out=logits[:, tiles, :],
+                in0=acc[:],
+                in1=bias_rows[:].unsqueeze(1).to_broadcast([P, GROUP, CLASSES]),
+                op=ALU.add,
+            )
+            nc.vector.scalar_tensor_tensor(
+                out=work[:, tiles, :], in0=logits[:, tiles, :], scalar=-1.0, in1=logits[:, tiles, :], op0=ALU.mult, op1=ALU.min
+            )
+            nc.scalar.activation(out=work[:, tiles, :], in_=work[:, tiles, :], func=ACT.Exp)
+
+        for g in range(GROUPS):
+            if g + 2 < GROUPS:
+                load_h(g + 2)
+            quantise_group(g)
+            if g >= 1:
+                logits_group(g - 1)
+        logits_group(GROUPS - 1)
+
+        def log1p_group(g):
+            tiles = group_tiles(g)
+            nc.scalar.activation(out=work[:, tiles, :], in_=work[:, tiles, :], func=ACT.Ln, bias=one[:], scale=1.0)
+
+        def evidence_group(g):
+            tiles = group_tiles(g)
+            nc.vector.scalar_tensor_tensor(
+                out=evidence[:, tiles, :], in0=logits[:, tiles, :], scalar=0.0, in1=work[:, tiles, :], op0=ALU.max, op1=ALU.add
+            )
+            nc.sync.dma_start(out=evidence_out[:, tiles, :], in_=evidence[:, tiles, :])
+            nc.vector.tensor_reduce(out=alpha_sum[:, tiles], in_=evidence[:, tiles, :], axis=AXIS_X, op=ALU.add)
+            nc.vector.tensor_scalar(
+                out=alpha_sum[:, tiles], in0=alpha_sum[:, tiles], scalar1=float(CLASSES), scalar2=None, op0=ALU.add
+            )
+            nc.vector.reciprocal(out=inv_sum[:, tiles], in_=alpha_sum[:, tiles])
+            for t in range(g * GROUP, (g + 1) * GROUP):
+                nc.scalar.activation(
+                    out=work[:, t, :], in_=evidence[:, t, :], func=ACT.Ln, bias=half_eps[:], scale=inv_sum[:, t : t + 1]
+                )
+
+        log1p_group(0)
+        for g in range(GROUPS):
+            if g + 1 < GROUPS:
+                log1p_group(g + 1)
+            evidence_group(g)
+        nc.vector.tensor_scalar(out=vacuity[:], in0=inv_sum[:], scalar1=float(CLASSES), scalar2=None, op0=ALU.mult)
+        nc.sync.dma_start(out=vacuity_out, in_=vacuity[:])
+
+        sorted_s = {}
+
+        def sort_group(g):
+            ping = sort_pool.tile([P, CLASSES, GROUP], F32)
+            pong = sort_pool.tile([P, CLASSES, GROUP], F32)
+            nc.vector.tensor_scalar(
+                out=ping[:], in0=work[:, group_tiles(g), :].rearrange("p t c -> p c t"), scalar1=0.5, scalar2=None, op0=ALU.mult
+            )
+            src, dst = ping, pong
+            for width_log in range(1, CLASS_BITS + 1):
+                for dist_log in reversed(range(width_log)):
+                    compare_exchange_stage(nc, src[:], dst[:], 2**width_log, 2**dist_log)
+                    src, dst = dst, src
+            s_sorted = pair_pool.tile([P, GROUP, CLASSES], F32)
+            nc.vector.tensor_copy(out=s_sorted[:], in_=src[:].rearrange("p c t -> p t c"))
+            sorted_s[g] = s_sorted
+
+        pair_results = {}
+
+        def pair_sums_group(g):
+            s_sorted = sorted_s[g]
+            shifted_belief = pair_pool.tile([P, GROUP, CLASSES], F32)
+            nc.scalar.activation(out=shifted_belief[:], in_=s_sorted[:], func=ACT.Exp, scale=2.0)
+            neg_tanh_sum = pair_pool.tile([P, GROUP, CLASSES], F32)
+            for t in range(GROUP):
+                unread = pair_pool.tile([P, PAIRS], F32)
+                column = 0
+                for i in range(CLASSES - 1):
+                    above = CLASSES - 1 - i
+                    nc.scalar.activation(
+                        out=unread[:, column : column + above],
+                        in_=s_sorted[:, t, i + 1 : CLASSES],
+                        func=ACT.Tanh,
+                        bias=s_sorted[:, t, i : i + 1],
+                        scale=-1.0,
+                        accum_out=neg_tanh_sum[:, t, i : i + 1],
+                    )
+                    column += above
+            pair_results[g] = (shifted_belief, neg_tanh_sum)
+
+        def outputs_group(g):
+            tiles = group_tiles(g)
+            alpha = out_pool.tile([P, GROUP, CLASSES], F32)
+            nc.vector.tensor_scalar(out=alpha[:], in0=evidence[:, tiles, :], scalar1=1.0, scalar2=None, op0=ALU.add)
+            nc.sync.dma_start(out=alpha_out[:, tiles, :], in_=alpha[:])
+            prob = out_pool.tile([P, GROUP, CLASSES], F32)
+            for t in range(GROUP):
+                nc.vector.tensor_scalar(
+                    out=prob[:, t, :], in0=alpha[:, t, :], scalar1=inv_sum[:, g * GROUP + t : g * GROUP + t + 1], scalar2=None, op0=ALU.mult
+                )
+            nc.sync.dma_start(out=prob_out[:, tiles, :], in_=prob[:])
+
+        def dissonance_group(g):
+            shifted_belief, neg_tanh_sum = pair_results[g]
+            lower = slice(0, CLASSES - 1)
+            xs = shifted_belief[:, :, lower]
+            count_term = out_pool.tile([P, GROUP, CLASSES], F32)
+            nc.vector.scalar_tensor_tensor(
+                out=count_term[:, :, lower],
+                in0=xs,
+                scalar=-EPS / 2,
+                in1=classes_above[:, lower].unsqueeze(1).to_broadcast([P, GROUP, CLASSES - 1]),
+                op0=ALU.add,
+                op1=ALU.mult,
+            )
+            tanh_term = out_pool.tile([P, GROUP, CLASSES], F32)
+            nc.vector.scalar_tensor_tensor(
+                out=tanh_term[:, :, lower], in0=xs, scalar=EPS / 2, in1=neg_tanh_sum[:, :, lower], op0=ALU.add, op1=ALU.mult
+            )
+            nc.vector.tensor_tensor(out=count_term[:, :, lower], in0=count_term[:, :, lower], in1=tanh_term[:, :, lower], op=ALU.subtract)
+            nc.vector.scalar_tensor_tensor(
+                out=tanh_term[:, :, lower], in0=xs, scalar=-EPS / 2, in1=count_term[:, :, lower], op0=ALU.add, op1=ALU.mult
+            )
+            nc.vector.tensor_reduce(out=dissonance[:, group_tiles(g)], in_=tanh_term[:, :, lower], axis=AXIS_X, op=ALU.add)
+
+        sort_group(0)
+        for g in range(GROUPS):
+            pair_sums_group(g)
+            outputs_group(g)
+            if g + 1 < GROUPS:
+                sort_group(g + 1)
+            dissonance_group(g)
+        nc.sync.dma_start(out=dissonance_out, in_=dissonance[:])

@@ -24,7 +24,11 @@ PASSES = K // 512
 TILES = ROWS // P
 GROUP = 4
 GROUPS = TILES // GROUP
-PAIRS = CLASSES * (CLASSES - 1) // 2
+TIP = 64
+TIP_BITS = 6
+DIRECT = CLASSES - TIP
+DIRECT_PAIRS = DIRECT * (CLASSES - 1) - DIRECT * (DIRECT - 1) // 2
+TIP_PAIRS = TIP * (TIP - 1) // 2
 
 FLOPS = 2 * ROWS * K * CLASSES
 
@@ -43,6 +47,19 @@ def compare_exchange_stage(nc, src, dst, width, dist):
         nc.vector.tensor_tensor(out=dst_view[:, :, d, :, 1, :], in0=low, in1=high, op=high_op)
 
 
+def tip_levels(differences):
+    levels = []
+    start = 0
+    for level in range(1, TIP_BITS + 1):
+        half = TIP // 2**level
+        blocks = TIP // (2 * half)
+        size = GROUP * blocks * half * half
+        part = differences[:, start : start + size].rearrange("p (t b i j) -> p t b i j", t=GROUP, b=blocks, i=half)
+        levels.append((half, blocks, part))
+        start += size
+    return levels
+
+
 def tile_evidentialhead_pb_kernel(tc, h_act, W3_words, W3_scales, b3, out_0, out_1, out_2, out_3, out_4):
     nc = tc.nc
     h_rows = h_act.rearrange("(p t) k -> p t k", t=TILES)
@@ -52,57 +69,14 @@ def tile_evidentialhead_pb_kernel(tc, h_act, W3_words, W3_scales, b3, out_0, out
     vacuity_out = out_3.rearrange("(p t) -> p t", t=TILES)
     dissonance_out = out_4.rearrange("(p t) -> p t", t=TILES)
 
+    def group_tiles(g):
+        return slice(g * GROUP, (g + 1) * GROUP)
+
     with ExitStack() as ctx:
         ctx.enter_context(tc.manual_schedule())
         const = ctx.enter_context(tc.tile_pool(name="const", bufs=1))
         whole = ctx.enter_context(tc.tile_pool(name="whole", bufs=1))
-        h_pool = ctx.enter_context(tc.tile_pool(name="h", bufs=3))
-        mx_pool = ctx.enter_context(tc.tile_pool(name="mx", bufs=2))
-        out_pool = ctx.enter_context(tc.tile_pool(name="outs", bufs=2))
-        sort_pool = ctx.enter_context(tc.tile_pool(name="sort", bufs=1))
-        pair_pool = ctx.enter_context(tc.tile_pool(name="pair", bufs=2))
-        psum_t = ctx.enter_context(tc.psum_pool(name="psum_t", bufs=6))
-        psum_l = ctx.enter_context(tc.psum_pool(name="psum_l", bufs=2))
 
-        def group_tiles(g):
-            return slice(g * GROUP, (g + 1) * GROUP)
-
-        h_tiles = {}
-
-        def load_h(g):
-            h_sb = h_pool.tile([P, GROUP, K], BF16, name="h_sb")
-            nc.sync.dma_start(out=h_sb[:], in_=h_rows[:, group_tiles(g), :])
-            h_tiles[g] = h_sb
-
-        load_h(0)
-        w_scales = const.tile([P, PASSES, CLASSES], U8, align_bytes=64)
-        nc.vector.memset(w_scales[:].bitcast(I32), 0)
-        w_words = const.tile([P, PASSES, 2 * CLASSES], U8, align_bytes=64)
-        for c in range(PASSES):
-            nc.sync.dma_start(out=w_words[:, c, :].bitcast(I32), in_=W3_words[c].bitcast(I32))
-            for quadrant in range(4):
-                nc.sync.dma_start(
-                    out=w_scales[32 * quadrant : 32 * quadrant + 4, c, :].bitcast(I32),
-                    in_=W3_scales[c, 4 * quadrant : 4 * quadrant + 4, :].bitcast(I32),
-                )
-        bias_rows = const.tile([P, CLASSES], BF16)
-        nc.sync.dma_start(out=bias_rows[:], in_=b3.partition_broadcast(P))
-        load_h(1)
-
-        identity = const.tile([P, P], F32)
-        make_identity(nc, identity[:])
-        class_index = const.tile([P, CLASSES], I32)
-        nc.gpsimd.iota(class_index[:], pattern=[[1, CLASSES]], base=0, channel_multiplier=0)
-        classes_above = const.tile([P, CLASSES], F32)
-        nc.vector.tensor_scalar(
-            out=classes_above[:], in0=class_index[:], scalar1=-1.0, scalar2=float(CLASSES - 1), op0=ALU.mult, op1=ALU.add
-        )
-        one = const.tile([P, 1], F32)
-        nc.vector.memset(one[:], 1.0)
-        half_eps = const.tile([P, 1], F32)
-        nc.vector.memset(half_eps[:], EPS / 2)
-
-        logits = whole.tile([P, TILES, CLASSES], F32)
         work = whole.tile([P, TILES, CLASSES], F32)
         evidence = whole.tile([P, TILES, CLASSES], F32)
         alpha_sum = whole.tile([P, TILES], F32)
@@ -110,94 +84,149 @@ def tile_evidentialhead_pb_kernel(tc, h_act, W3_words, W3_scales, b3, out_0, out
         vacuity = whole.tile([P, TILES], F32)
         dissonance = whole.tile([P, TILES], F32)
 
-        mx_operands = {}
+        with ExitStack() as head:
+            h_pool = head.enter_context(tc.tile_pool(name="h", bufs=3))
+            mx_pool = head.enter_context(tc.tile_pool(name="mx", bufs=2))
+            logit_pool = head.enter_context(tc.tile_pool(name="logit", bufs=1))
+            psum_t = head.enter_context(tc.psum_pool(name="psum_t", bufs=6))
+            psum_l = head.enter_context(tc.psum_pool(name="psum_l", bufs=2))
 
-        def quantise_group(g):
-            h_sb = h_tiles[g]
-            grouped = mx_pool.tile([P, GROUP, K], BF16, align_bytes=64)
-            for t in range(GROUP):
-                h_words = h_sb[:, t, :].bitcast(F32)
-                flipped = psum_t.tile([P, PASSES, 2, P], F32)
-                for c in range(PASSES):
-                    for u in range(2):
-                        nc.tensor.transpose(flipped[:, c, u, :], h_words[:, 256 * c + u : 256 * (c + 1) : 2], identity[:])
-                nc.scalar.copy(
-                    out=grouped[:, t, :].bitcast(F32).rearrange("p (c r u) -> p c r u", c=PASSES, u=2),
-                    in_=flipped[:].rearrange("p c u r -> p c r u"),
-                )
-            codes = mx_pool.tile([P, GROUP, PASSES * P], U32, align_bytes=64)
-            scales = mx_pool.tile([P, GROUP, PASSES * P], U8, align_bytes=64)
-            nc.vector.quantize_mx(
-                out=codes[:].rearrange("p t w -> p (t w)").bitcast(FP8X4),
-                scales=scales[:].rearrange("p t w -> p (t w)"),
-                in_=grouped[:].rearrange("p t k -> p (t k)"),
-            )
-            mx_operands[g] = (codes, scales)
+            h_tiles = {}
 
-        def logits_group(g):
-            codes, scales = mx_operands[g]
-            acc = psum_l.tile([P, GROUP, CLASSES], F32)
-            for t in range(GROUP):
-                for c in range(PASSES):
-                    rows = slice(c * P, (c + 1) * P)
-                    nc.tensor.matmul_mx(
-                        out=acc[:, t, :],
-                        lhsT=codes[:, t, rows].bitcast(FP8X4),
-                        lhsT_scale=scales[:, t, rows],
-                        rhs=w_words[:, c, :].bitcast(FP4X4),
-                        rhs_scale=w_scales[:, c, :],
-                        start=(c == 0),
-                        stop=(c == PASSES - 1),
+            def load_h(g):
+                h_sb = h_pool.tile([P, GROUP, K], BF16, name="h_sb")
+                nc.sync.dma_start(out=h_sb[:], in_=h_rows[:, group_tiles(g), :])
+                h_tiles[g] = h_sb
+
+            load_h(0)
+            w_scales = const.tile([P, PASSES, CLASSES], U8, align_bytes=64)
+            nc.vector.memset(w_scales[:].bitcast(I32), 0)
+            w_words = const.tile([P, PASSES, 2 * CLASSES], U8, align_bytes=64)
+            for c in range(PASSES):
+                nc.sync.dma_start(out=w_words[:, c, :].bitcast(I32), in_=W3_words[c].bitcast(I32))
+                for quadrant in range(4):
+                    nc.sync.dma_start(
+                        out=w_scales[32 * quadrant : 32 * quadrant + 4, c, :].bitcast(I32),
+                        in_=W3_scales[c, 4 * quadrant : 4 * quadrant + 4, :].bitcast(I32),
                     )
-            tiles = group_tiles(g)
-            nc.vector.tensor_tensor(
-                out=logits[:, tiles, :],
-                in0=acc[:],
-                in1=bias_rows[:].unsqueeze(1).to_broadcast([P, GROUP, CLASSES]),
-                op=ALU.add,
-            )
-            nc.vector.scalar_tensor_tensor(
-                out=work[:, tiles, :], in0=logits[:, tiles, :], scalar=-1.0, in1=logits[:, tiles, :], op0=ALU.mult, op1=ALU.min
-            )
-            nc.scalar.activation(out=work[:, tiles, :], in_=work[:, tiles, :], func=ACT.Exp)
+            bias_rows = const.tile([P, CLASSES], BF16)
+            nc.sync.dma_start(out=bias_rows[:], in_=b3.partition_broadcast(P))
+            load_h(1)
 
-        for g in range(GROUPS):
-            if g + 2 < GROUPS:
-                load_h(g + 2)
-            quantise_group(g)
-            if g >= 1:
-                logits_group(g - 1)
-        logits_group(GROUPS - 1)
-
-        def log1p_group(g):
-            tiles = group_tiles(g)
-            nc.scalar.activation(out=work[:, tiles, :], in_=work[:, tiles, :], func=ACT.Ln, bias=one[:], scale=1.0)
-
-        def evidence_group(g):
-            tiles = group_tiles(g)
-            nc.vector.scalar_tensor_tensor(
-                out=evidence[:, tiles, :], in0=logits[:, tiles, :], scalar=0.0, in1=work[:, tiles, :], op0=ALU.max, op1=ALU.add
-            )
-            nc.sync.dma_start(out=evidence_out[:, tiles, :], in_=evidence[:, tiles, :])
-            nc.vector.tensor_reduce(out=alpha_sum[:, tiles], in_=evidence[:, tiles, :], axis=AXIS_X, op=ALU.add)
+            identity = const.tile([P, P], F32)
+            make_identity(nc, identity[:])
+            class_index = const.tile([P, CLASSES], I32)
+            nc.gpsimd.iota(class_index[:], pattern=[[1, CLASSES]], base=0, channel_multiplier=0)
+            classes_above = const.tile([P, CLASSES], F32)
             nc.vector.tensor_scalar(
-                out=alpha_sum[:, tiles], in0=alpha_sum[:, tiles], scalar1=float(CLASSES), scalar2=None, op0=ALU.add
+                out=classes_above[:], in0=class_index[:], scalar1=-1.0, scalar2=float(CLASSES - 1), op0=ALU.mult, op1=ALU.add
             )
-            nc.vector.reciprocal(out=inv_sum[:, tiles], in_=alpha_sum[:, tiles])
-            for t in range(g * GROUP, (g + 1) * GROUP):
-                nc.scalar.activation(
-                    out=work[:, t, :], in_=evidence[:, t, :], func=ACT.Ln, bias=half_eps[:], scale=inv_sum[:, t : t + 1]
-                )
+            one = const.tile([P, 1], F32)
+            nc.vector.memset(one[:], 1.0)
+            half_eps = const.tile([P, 1], F32)
+            nc.vector.memset(half_eps[:], EPS / 2)
 
-        log1p_group(0)
-        for g in range(GROUPS):
-            if g + 1 < GROUPS:
-                log1p_group(g + 1)
-            evidence_group(g)
-        nc.vector.tensor_scalar(out=vacuity[:], in0=inv_sum[:], scalar1=float(CLASSES), scalar2=None, op0=ALU.mult)
-        nc.sync.dma_start(out=vacuity_out, in_=vacuity[:])
+            logits = logit_pool.tile([P, TILES, CLASSES], F32)
+
+            grouped_tiles = {}
+            mx_operands = {}
+
+            def flip_group(g):
+                h_sb = h_tiles[g]
+                grouped = mx_pool.tile([P, GROUP, K], BF16, align_bytes=64)
+                for t in range(GROUP):
+                    h_words = h_sb[:, t, :].bitcast(F32)
+                    flipped = psum_t.tile([P, PASSES, 2, P], F32)
+                    for c in range(PASSES):
+                        for u in range(2):
+                            nc.tensor.transpose(flipped[:, c, u, :], h_words[:, 256 * c + u : 256 * (c + 1) : 2], identity[:])
+                    nc.scalar.copy(
+                        out=grouped[:, t, :].bitcast(F32).rearrange("p (c r u) -> p c r u", c=PASSES, u=2),
+                        in_=flipped[:].rearrange("p c u r -> p c r u"),
+                    )
+                grouped_tiles[g] = grouped
+
+            def quantise_group(g):
+                codes = mx_pool.tile([P, GROUP, PASSES * P], U32, align_bytes=64)
+                scales = mx_pool.tile([P, GROUP, PASSES * P], U8, align_bytes=64)
+                nc.vector.quantize_mx(
+                    out=codes[:].rearrange("p t w -> p (t w)").bitcast(FP8X4),
+                    scales=scales[:].rearrange("p t w -> p (t w)"),
+                    in_=grouped_tiles[g][:].rearrange("p t k -> p (t k)"),
+                )
+                mx_operands[g] = (codes, scales)
+
+            def logits_group(g):
+                codes, scales = mx_operands[g]
+                acc = psum_l.tile([P, GROUP, CLASSES], F32)
+                for t in range(GROUP):
+                    for c in range(PASSES):
+                        rows = slice(c * P, (c + 1) * P)
+                        nc.tensor.matmul_mx(
+                            out=acc[:, t, :],
+                            lhsT=codes[:, t, rows].bitcast(FP8X4),
+                            lhsT_scale=scales[:, t, rows],
+                            rhs=w_words[:, c, :].bitcast(FP4X4),
+                            rhs_scale=w_scales[:, c, :],
+                            start=(c == 0),
+                            stop=(c == PASSES - 1),
+                        )
+                tiles = group_tiles(g)
+                nc.vector.tensor_tensor(
+                    out=logits[:, tiles, :],
+                    in0=acc[:],
+                    in1=bias_rows[:].unsqueeze(1).to_broadcast([P, GROUP, CLASSES]),
+                    op=ALU.add,
+                )
+                nc.vector.scalar_tensor_tensor(
+                    out=work[:, tiles, :], in0=logits[:, tiles, :], scalar=-1.0, in1=logits[:, tiles, :], op0=ALU.mult, op1=ALU.min
+                )
+                nc.scalar.activation(out=work[:, tiles, :], in_=work[:, tiles, :], func=ACT.Exp)
+
+            for g in range(GROUPS):
+                if g + 2 < GROUPS:
+                    load_h(g + 2)
+                flip_group(g)
+                if g >= 1:
+                    logits_group(g - 1)
+                quantise_group(g)
+            logits_group(GROUPS - 1)
+
+            def log1p_group(g):
+                tiles = group_tiles(g)
+                nc.scalar.activation(out=work[:, tiles, :], in_=work[:, tiles, :], func=ACT.Ln, bias=one[:], scale=1.0)
+
+            def evidence_group(g):
+                tiles = group_tiles(g)
+                nc.vector.scalar_tensor_tensor(
+                    out=evidence[:, tiles, :], in0=logits[:, tiles, :], scalar=0.0, in1=work[:, tiles, :], op0=ALU.max, op1=ALU.add
+                )
+                nc.sync.dma_start(out=evidence_out[:, tiles, :], in_=evidence[:, tiles, :])
+                nc.vector.tensor_reduce(out=alpha_sum[:, tiles], in_=evidence[:, tiles, :], axis=AXIS_X, op=ALU.add)
+                nc.vector.tensor_scalar(
+                    out=alpha_sum[:, tiles], in0=alpha_sum[:, tiles], scalar1=float(CLASSES), scalar2=None, op0=ALU.add
+                )
+                nc.vector.reciprocal(out=inv_sum[:, tiles], in_=alpha_sum[:, tiles])
+                for t in range(g * GROUP, (g + 1) * GROUP):
+                    nc.scalar.activation(
+                        out=work[:, t, :], in_=evidence[:, t, :], func=ACT.Ln, bias=half_eps[:], scale=inv_sum[:, t : t + 1]
+                    )
+
+            log1p_group(0)
+            for g in range(GROUPS):
+                if g + 1 < GROUPS:
+                    log1p_group(g + 1)
+                evidence_group(g)
+            nc.vector.tensor_scalar(out=vacuity[:], in0=inv_sum[:], scalar1=float(CLASSES), scalar2=None, op0=ALU.mult)
+            nc.sync.dma_start(out=vacuity_out, in_=vacuity[:])
+
+        out_pool = ctx.enter_context(tc.tile_pool(name="outs", bufs=2))
+        sort_pool = ctx.enter_context(tc.tile_pool(name="sort", bufs=1))
+        pair_pool = ctx.enter_context(tc.tile_pool(name="pair", bufs=2))
 
         sorted_s = {}
+        tip_tiles = {}
+        pair_results = {}
 
         def sort_group(g):
             ping = sort_pool.tile([P, CLASSES, GROUP], F32)
@@ -214,28 +243,72 @@ def tile_evidentialhead_pb_kernel(tc, h_act, W3_words, W3_scales, b3, out_0, out
             nc.vector.tensor_copy(out=s_sorted[:], in_=src[:].rearrange("p c t -> p t c"))
             sorted_s[g] = s_sorted
 
-        pair_results = {}
+        def tip_differences(g):
+            differences = pair_pool.tile([P, GROUP * TIP_PAIRS], F32)
+            for half, blocks, part in tip_levels(differences):
+                halves = sorted_s[g][:, :, DIRECT:CLASSES].rearrange("p t (b s i) -> p t b s i", b=blocks, s=2)
+                lower = halves[:, :, :, 0, :]
+                upper = halves[:, :, :, 1, :]
+                if blocks <= half:
+                    for b in range(blocks):
+                        nc.vector.tensor_tensor(
+                            out=part[:, :, b, :, :],
+                            in0=lower[:, :, b, :].unsqueeze(3).to_broadcast([P, GROUP, half, half]),
+                            in1=upper[:, :, b, :].unsqueeze(2).to_broadcast([P, GROUP, half, half]),
+                            op=ALU.subtract,
+                        )
+                else:
+                    for i in range(half):
+                        nc.vector.tensor_tensor(
+                            out=part[:, :, :, i, :],
+                            in0=lower[:, :, :, i : i + 1].to_broadcast([P, GROUP, blocks, half]),
+                            in1=upper,
+                            op=ALU.subtract,
+                        )
+            tip_tiles[g] = differences
+
+        def direct_sums(s_sorted, neg_tanh_sum, t):
+            unread = pair_pool.tile([P, DIRECT_PAIRS], F32)
+            column = 0
+            for i in range(DIRECT):
+                above = CLASSES - 1 - i
+                nc.scalar.activation(
+                    out=unread[:, column : column + above],
+                    in_=s_sorted[:, t, i + 1 : CLASSES],
+                    func=ACT.Tanh,
+                    bias=s_sorted[:, t, i : i + 1],
+                    scale=-1.0,
+                    accum_out=neg_tanh_sum[:, t, i : i + 1],
+                )
+                column += above
 
         def pair_sums_group(g):
             s_sorted = sorted_s[g]
             shifted_belief = pair_pool.tile([P, GROUP, CLASSES], F32)
             nc.scalar.activation(out=shifted_belief[:], in_=s_sorted[:], func=ACT.Exp, scale=2.0)
             neg_tanh_sum = pair_pool.tile([P, GROUP, CLASSES], F32)
-            for t in range(GROUP):
-                unread = pair_pool.tile([P, PAIRS], F32)
-                column = 0
-                for i in range(CLASSES - 1):
-                    above = CLASSES - 1 - i
-                    nc.scalar.activation(
-                        out=unread[:, column : column + above],
-                        in_=s_sorted[:, t, i + 1 : CLASSES],
-                        func=ACT.Tanh,
-                        bias=s_sorted[:, t, i : i + 1],
-                        scale=-1.0,
-                        accum_out=neg_tanh_sum[:, t, i : i + 1],
-                    )
-                    column += above
+            direct_sums(s_sorted, neg_tanh_sum, 0)
+            nc.scalar.activation(out=tip_tiles[g][:], in_=tip_tiles[g][:], func=ACT.Tanh)
+            for t in range(1, GROUP):
+                direct_sums(s_sorted, neg_tanh_sum, t)
             pair_results[g] = (shifted_belief, neg_tanh_sum)
+
+        def tip_sums(g):
+            neg_tanh_sum = pair_results[g][1]
+            nc.vector.memset(neg_tanh_sum[:, :, DIRECT:CLASSES], 0.0)
+            level_sums = pair_pool.tile([P, TIP_BITS, GROUP * TIP // 2], F32)
+            for level, (half, blocks, part) in enumerate(tip_levels(tip_tiles[g])):
+                nc.vector.tensor_reduce(
+                    out=level_sums[:, level, :], in_=part.rearrange("p t b i j -> p (t b i) j"), axis=AXIS_X, op=ALU.add
+                )
+            for level, (half, blocks, part) in enumerate(tip_levels(tip_tiles[g])):
+                lower = neg_tanh_sum[:, :, DIRECT:CLASSES].rearrange("p t (b s i) -> p t b s i", b=blocks, s=2)[:, :, :, 0, :]
+                nc.vector.tensor_tensor(
+                    out=lower,
+                    in0=lower,
+                    in1=level_sums[:, level, :].rearrange("p (t b i) -> p t b i", t=GROUP, b=blocks),
+                    op=ALU.add,
+                )
 
         def outputs_group(g):
             tiles = group_tiles(g)
@@ -251,32 +324,33 @@ def tile_evidentialhead_pb_kernel(tc, h_act, W3_words, W3_scales, b3, out_0, out
 
         def dissonance_group(g):
             shifted_belief, neg_tanh_sum = pair_results[g]
-            lower = slice(0, CLASSES - 1)
-            xs = shifted_belief[:, :, lower]
             count_term = out_pool.tile([P, GROUP, CLASSES], F32)
             nc.vector.scalar_tensor_tensor(
-                out=count_term[:, :, lower],
-                in0=xs,
+                out=count_term[:],
+                in0=shifted_belief[:],
                 scalar=-EPS / 2,
-                in1=classes_above[:, lower].unsqueeze(1).to_broadcast([P, GROUP, CLASSES - 1]),
+                in1=classes_above[:].unsqueeze(1).to_broadcast([P, GROUP, CLASSES]),
                 op0=ALU.add,
                 op1=ALU.mult,
             )
             tanh_term = out_pool.tile([P, GROUP, CLASSES], F32)
             nc.vector.scalar_tensor_tensor(
-                out=tanh_term[:, :, lower], in0=xs, scalar=EPS / 2, in1=neg_tanh_sum[:, :, lower], op0=ALU.add, op1=ALU.mult
+                out=tanh_term[:], in0=shifted_belief[:], scalar=EPS / 2, in1=neg_tanh_sum[:], op0=ALU.add, op1=ALU.mult
             )
-            nc.vector.tensor_tensor(out=count_term[:, :, lower], in0=count_term[:, :, lower], in1=tanh_term[:, :, lower], op=ALU.subtract)
+            nc.vector.tensor_tensor(out=count_term[:], in0=count_term[:], in1=tanh_term[:], op=ALU.subtract)
             nc.vector.scalar_tensor_tensor(
-                out=tanh_term[:, :, lower], in0=xs, scalar=-EPS / 2, in1=count_term[:, :, lower], op0=ALU.add, op1=ALU.mult
+                out=tanh_term[:], in0=shifted_belief[:], scalar=-EPS / 2, in1=count_term[:], op0=ALU.add, op1=ALU.mult
             )
-            nc.vector.tensor_reduce(out=dissonance[:, group_tiles(g)], in_=tanh_term[:, :, lower], axis=AXIS_X, op=ALU.add)
+            nc.vector.tensor_reduce(out=dissonance[:, group_tiles(g)], in_=tanh_term[:], axis=AXIS_X, op=ALU.add)
 
         sort_group(0)
+        tip_differences(0)
         for g in range(GROUPS):
             pair_sums_group(g)
             outputs_group(g)
             if g + 1 < GROUPS:
                 sort_group(g + 1)
+                tip_differences(g + 1)
+            tip_sums(g)
             dissonance_group(g)
         nc.sync.dma_start(out=dissonance_out, in_=dissonance[:])

@@ -34,13 +34,17 @@ FLOPS = 2 * ROWS * K * CLASSES
 
 
 def compare_exchange_stage(nc, src, dst, width, dist):
-    directions = 2 if width < CLASSES else 1
+    if dist == CLASSES // 2:
+        parts, run = 1, CLASSES
+    else:
+        parts, run = 2, min(width, CLASSES // 2)
     pattern = "p (a d b s j) g -> p a d b s (j g)"
-    sizes = dict(a=CLASSES // (width * directions), d=directions, b=width // (2 * dist), s=2, j=dist)
+    sizes = dict(a=CLASSES // (run * parts), d=parts, b=run // (2 * dist), s=2, j=dist)
     src_view = src.rearrange(pattern, **sizes)
     dst_view = dst.rearrange(pattern, **sizes)
-    for d in range(directions):
-        low_op, high_op = (ALU.min, ALU.max) if d == 0 else (ALU.max, ALU.min)
+    for d in range(parts):
+        falling = width < CLASSES and d == 1
+        low_op, high_op = (ALU.max, ALU.min) if falling else (ALU.min, ALU.max)
         low = src_view[:, :, d, :, 0, :]
         high = src_view[:, :, d, :, 1, :]
         nc.vector.tensor_tensor(out=dst_view[:, :, d, :, 0, :], in0=low, in1=high, op=low_op)
@@ -83,6 +87,10 @@ def tile_evidentialhead_pb_kernel(tc, h_act, W3_words, W3_scales, b3, out_0, out
         inv_sum = whole.tile([P, TILES], F32)
         vacuity = whole.tile([P, TILES], F32)
         dissonance = whole.tile([P, TILES], F32)
+
+        out_pool = ctx.enter_context(tc.tile_pool(name="outs", bufs=2))
+        sort_pool = ctx.enter_context(tc.tile_pool(name="sort", bufs=1))
+        pair_pool = ctx.enter_context(tc.tile_pool(name="pair", bufs=2))
 
         with ExitStack() as head:
             h_pool = head.enter_context(tc.tile_pool(name="h", bufs=3))
@@ -127,6 +135,8 @@ def tile_evidentialhead_pb_kernel(tc, h_act, W3_words, W3_scales, b3, out_0, out
             nc.vector.memset(half_eps[:], EPS / 2)
 
             logits = logit_pool.tile([P, TILES, CLASSES], F32)
+            alpha = logit_pool.tile([P, TILES, CLASSES], F32)
+            prob = logit_pool.tile([P, TILES, CLASSES], F32)
 
             grouped_tiles = {}
             mx_operands = {}
@@ -192,37 +202,34 @@ def tile_evidentialhead_pb_kernel(tc, h_act, W3_words, W3_scales, b3, out_0, out
                 quantise_group(g)
             logits_group(GROUPS - 1)
 
-            def log1p_group(g):
+            for g in range(GROUPS):
                 tiles = group_tiles(g)
                 nc.scalar.activation(out=work[:, tiles, :], in_=work[:, tiles, :], func=ACT.Ln, bias=one[:], scale=1.0)
-
-            def evidence_group(g):
-                tiles = group_tiles(g)
                 nc.vector.scalar_tensor_tensor(
                     out=evidence[:, tiles, :], in0=logits[:, tiles, :], scalar=0.0, in1=work[:, tiles, :], op0=ALU.max, op1=ALU.add
                 )
                 nc.sync.dma_start(out=evidence_out[:, tiles, :], in_=evidence[:, tiles, :])
-                nc.vector.tensor_reduce(out=alpha_sum[:, tiles], in_=evidence[:, tiles, :], axis=AXIS_X, op=ALU.add)
-                nc.vector.tensor_scalar(
-                    out=alpha_sum[:, tiles], in0=alpha_sum[:, tiles], scalar1=float(CLASSES), scalar2=None, op0=ALU.add
-                )
-                nc.vector.reciprocal(out=inv_sum[:, tiles], in_=alpha_sum[:, tiles])
+            for g in range(GROUPS):
                 for t in range(g * GROUP, (g + 1) * GROUP):
                     nc.scalar.activation(
-                        out=work[:, t, :], in_=evidence[:, t, :], func=ACT.Ln, bias=half_eps[:], scale=inv_sum[:, t : t + 1]
+                        out=alpha[:, t, :], in_=evidence[:, t, :], func=ACT.Identity, bias=one[:], scale=1.0, accum_out=alpha_sum[:, t : t + 1]
                     )
-
-            log1p_group(0)
-            for g in range(GROUPS):
-                if g + 1 < GROUPS:
-                    log1p_group(g + 1)
-                evidence_group(g)
+                nc.sync.dma_start(out=alpha_out[:, group_tiles(g), :], in_=alpha[:, group_tiles(g), :])
+            nc.vector.reciprocal(out=inv_sum[:], in_=alpha_sum[:])
             nc.vector.tensor_scalar(out=vacuity[:], in0=inv_sum[:], scalar1=float(CLASSES), scalar2=None, op0=ALU.mult)
             nc.sync.dma_start(out=vacuity_out, in_=vacuity[:])
+            for t in range(TILES):
+                nc.scalar.activation(
+                    out=work[:, t, :], in_=evidence[:, t, :], func=ACT.Ln, bias=half_eps[:], scale=inv_sum[:, t : t + 1]
+                )
+            for g in range(GROUPS):
+                for t in range(g * GROUP, (g + 1) * GROUP):
+                    nc.scalar.activation(
+                        out=prob[:, t, :], in_=evidence[:, t, :], func=ACT.Identity, bias=inv_sum[:, t : t + 1], scale=inv_sum[:, t : t + 1]
+                    )
+                nc.sync.dma_start(out=prob_out[:, group_tiles(g), :], in_=prob[:, group_tiles(g), :])
 
-        out_pool = ctx.enter_context(tc.tile_pool(name="outs", bufs=2))
-        sort_pool = ctx.enter_context(tc.tile_pool(name="sort", bufs=1))
-        pair_pool = ctx.enter_context(tc.tile_pool(name="pair", bufs=2))
+        large_pool = ctx.enter_context(tc.tile_pool(name="large", bufs=2))
 
         sorted_s = {}
         tip_tiles = {}
@@ -244,7 +251,7 @@ def tile_evidentialhead_pb_kernel(tc, h_act, W3_words, W3_scales, b3, out_0, out
             sorted_s[g] = s_sorted
 
         def tip_differences(g):
-            differences = pair_pool.tile([P, GROUP * TIP_PAIRS], F32)
+            differences = large_pool.tile([P, GROUP * TIP_PAIRS], F32)
             for half, blocks, part in tip_levels(differences):
                 halves = sorted_s[g][:, :, DIRECT:CLASSES].rearrange("p t (b s i) -> p t b s i", b=blocks, s=2)
                 lower = halves[:, :, :, 0, :]
@@ -268,7 +275,7 @@ def tile_evidentialhead_pb_kernel(tc, h_act, W3_words, W3_scales, b3, out_0, out
             tip_tiles[g] = differences
 
         def direct_sums(s_sorted, neg_tanh_sum, t):
-            unread = pair_pool.tile([P, DIRECT_PAIRS], F32)
+            unread = large_pool.tile([P, DIRECT_PAIRS], F32)
             column = 0
             for i in range(DIRECT):
                 above = CLASSES - 1 - i
@@ -310,18 +317,6 @@ def tile_evidentialhead_pb_kernel(tc, h_act, W3_words, W3_scales, b3, out_0, out
                     op=ALU.add,
                 )
 
-        def outputs_group(g):
-            tiles = group_tiles(g)
-            alpha = out_pool.tile([P, GROUP, CLASSES], F32)
-            nc.vector.tensor_scalar(out=alpha[:], in0=evidence[:, tiles, :], scalar1=1.0, scalar2=None, op0=ALU.add)
-            nc.sync.dma_start(out=alpha_out[:, tiles, :], in_=alpha[:])
-            prob = out_pool.tile([P, GROUP, CLASSES], F32)
-            for t in range(GROUP):
-                nc.vector.tensor_scalar(
-                    out=prob[:, t, :], in0=alpha[:, t, :], scalar1=inv_sum[:, g * GROUP + t : g * GROUP + t + 1], scalar2=None, op0=ALU.mult
-                )
-            nc.sync.dma_start(out=prob_out[:, tiles, :], in_=prob[:])
-
         def dissonance_group(g):
             shifted_belief, neg_tanh_sum = pair_results[g]
             count_term = out_pool.tile([P, GROUP, CLASSES], F32)
@@ -347,7 +342,6 @@ def tile_evidentialhead_pb_kernel(tc, h_act, W3_words, W3_scales, b3, out_0, out
         tip_differences(0)
         for g in range(GROUPS):
             pair_sums_group(g)
-            outputs_group(g)
             if g + 1 < GROUPS:
                 sort_group(g + 1)
                 tip_differences(g + 1)

@@ -24,11 +24,13 @@ PASSES = K // 512
 TILES = ROWS // P
 GROUP = 4
 GROUPS = TILES // GROUP
-TIP = 64
-TIP_BITS = 6
+STEP = 8
+STEP_BITS = 3
+TIP = 72
 DIRECT = CLASSES - TIP
 DIRECT_PAIRS = DIRECT * (CLASSES - 1) - DIRECT * (DIRECT - 1) // 2
 TIP_PAIRS = TIP * (TIP - 1) // 2
+PAIR_GROUPS = [(0, GROUP // 2), (GROUP // 2, GROUP // 2)] + [(first, GROUP) for first in range(GROUP, TILES, GROUP)]
 
 FLOPS = 2 * ROWS * K * CLASSES
 
@@ -51,17 +53,23 @@ def compare_exchange_stage(nc, src, dst, width, dist):
         nc.vector.tensor_tensor(out=dst_view[:, :, d, :, 1, :], in0=low, in1=high, op=high_op)
 
 
-def tip_levels(differences):
-    levels = []
+def tip_parts(differences, count):
+    rectangles = []
+    squares = []
     start = 0
-    for level in range(1, TIP_BITS + 1):
-        half = TIP // 2**level
-        blocks = TIP // (2 * half)
-        size = GROUP * blocks * half * half
-        part = differences[:, start : start + size].rearrange("p (t b i j) -> p t b i j", t=GROUP, b=blocks, i=half)
-        levels.append((half, blocks, part))
+    for first in range(DIRECT, CLASSES - STEP, STEP):
+        above = CLASSES - first - STEP
+        size = count * STEP * above
+        piece = differences[:, start : start + size].rearrange("p (t i j) -> p t i j", t=count, i=STEP)
+        rectangles.append((slice(first, first + STEP), slice(first + STEP, CLASSES), piece))
         start += size
-    return levels
+    for level in range(1, STEP_BITS + 1):
+        half = STEP // 2**level
+        size = count * (TIP // 2) * half
+        piece = differences[:, start : start + size].rearrange("p (t b i j) -> p t b i j", t=count, i=half, j=half)
+        squares.append((half, piece))
+        start += size
+    return rectangles, squares
 
 
 def tile_evidentialhead_pb_kernel(tc, h_act, W3_words, W3_scales, b3, out_0, out_1, out_2, out_3, out_4):
@@ -150,7 +158,8 @@ def tile_evidentialhead_pb_kernel(tc, h_act, W3_words, W3_scales, b3, out_0, out
                     for c in range(PASSES):
                         for u in range(2):
                             nc.tensor.transpose(flipped[:, c, u, :], h_words[:, 256 * c + u : 256 * (c + 1) : 2], identity[:])
-                    nc.scalar.copy(
+                    copy_out = nc.vector.tensor_copy if t == GROUP - 1 else nc.scalar.copy
+                    copy_out(
                         out=grouped[:, t, :].bitcast(F32).rearrange("p (c r u) -> p c r u", c=PASSES, u=2),
                         in_=flipped[:].rearrange("p c u r -> p c r u"),
                     )
@@ -191,16 +200,22 @@ def tile_evidentialhead_pb_kernel(tc, h_act, W3_words, W3_scales, b3, out_0, out
                 nc.vector.scalar_tensor_tensor(
                     out=work[:, tiles, :], in0=logits[:, tiles, :], scalar=-1.0, in1=logits[:, tiles, :], op0=ALU.mult, op1=ALU.min
                 )
+
+            def exp_group(g):
+                tiles = group_tiles(g)
                 nc.scalar.activation(out=work[:, tiles, :], in_=work[:, tiles, :], func=ACT.Exp)
 
-            for g in range(GROUPS):
+            for g in range(GROUPS + 2):
                 if g + 2 < GROUPS:
                     load_h(g + 2)
-                flip_group(g)
-                if g >= 1:
+                if g < GROUPS:
+                    flip_group(g)
+                if 1 <= g <= GROUPS:
                     logits_group(g - 1)
-                quantise_group(g)
-            logits_group(GROUPS - 1)
+                if g < GROUPS:
+                    quantise_group(g)
+                if g >= 2:
+                    exp_group(g - 2)
 
             for g in range(GROUPS):
                 tiles = group_tiles(g)
@@ -235,44 +250,44 @@ def tile_evidentialhead_pb_kernel(tc, h_act, W3_words, W3_scales, b3, out_0, out
         tip_tiles = {}
         pair_results = {}
 
-        def sort_group(g):
-            ping = sort_pool.tile([P, CLASSES, GROUP], F32)
-            pong = sort_pool.tile([P, CLASSES, GROUP], F32)
+        def sort_group(n):
+            first, count = PAIR_GROUPS[n]
+            ping = sort_pool.tile([P, CLASSES, count], F32)
+            pong = sort_pool.tile([P, CLASSES, count], F32)
             nc.vector.tensor_scalar(
-                out=ping[:], in0=work[:, group_tiles(g), :].rearrange("p t c -> p c t"), scalar1=0.5, scalar2=None, op0=ALU.mult
+                out=ping[:], in0=work[:, first : first + count, :].rearrange("p t c -> p c t"), scalar1=0.5, scalar2=None, op0=ALU.mult
             )
             src, dst = ping, pong
             for width_log in range(1, CLASS_BITS + 1):
                 for dist_log in reversed(range(width_log)):
                     compare_exchange_stage(nc, src[:], dst[:], 2**width_log, 2**dist_log)
                     src, dst = dst, src
-            s_sorted = pair_pool.tile([P, GROUP, CLASSES], F32)
+            s_sorted = pair_pool.tile([P, count, CLASSES], F32)
             nc.vector.tensor_copy(out=s_sorted[:], in_=src[:].rearrange("p c t -> p t c"))
-            sorted_s[g] = s_sorted
+            sorted_s[n] = s_sorted
 
-        def tip_differences(g):
-            differences = large_pool.tile([P, GROUP * TIP_PAIRS], F32)
-            for half, blocks, part in tip_levels(differences):
-                halves = sorted_s[g][:, :, DIRECT:CLASSES].rearrange("p t (b s i) -> p t b s i", b=blocks, s=2)
-                lower = halves[:, :, :, 0, :]
-                upper = halves[:, :, :, 1, :]
-                if blocks <= half:
-                    for b in range(blocks):
-                        nc.vector.tensor_tensor(
-                            out=part[:, :, b, :, :],
-                            in0=lower[:, :, b, :].unsqueeze(3).to_broadcast([P, GROUP, half, half]),
-                            in1=upper[:, :, b, :].unsqueeze(2).to_broadcast([P, GROUP, half, half]),
-                            op=ALU.subtract,
-                        )
-                else:
-                    for i in range(half):
-                        nc.vector.tensor_tensor(
-                            out=part[:, :, :, i, :],
-                            in0=lower[:, :, :, i : i + 1].to_broadcast([P, GROUP, blocks, half]),
-                            in1=upper,
-                            op=ALU.subtract,
-                        )
-            tip_tiles[g] = differences
+        def tip_differences(n):
+            count = PAIR_GROUPS[n][1]
+            s_sorted = sorted_s[n]
+            differences = large_pool.tile([P, count * TIP_PAIRS], F32)
+            rectangles, squares = tip_parts(differences, count)
+            for classes_i, classes_j, piece in rectangles:
+                nc.vector.tensor_tensor(
+                    out=piece,
+                    in0=s_sorted[:, :, classes_i].unsqueeze(3).to_broadcast(piece.shape),
+                    in1=s_sorted[:, :, classes_j].unsqueeze(2).to_broadcast(piece.shape),
+                    op=ALU.subtract,
+                )
+            for half, piece in squares:
+                halves = s_sorted[:, :, DIRECT:CLASSES].rearrange("p t (b s i) -> p t b s i", s=2, i=half)
+                for i in range(half):
+                    nc.vector.tensor_tensor(
+                        out=piece[:, :, :, i, :],
+                        in0=halves[:, :, :, 0, i : i + 1].to_broadcast(piece[:, :, :, i, :].shape),
+                        in1=halves[:, :, :, 1, :],
+                        op=ALU.subtract,
+                    )
+            tip_tiles[n] = differences
 
         def direct_sums(s_sorted, neg_tanh_sum, t):
             unread = large_pool.tile([P, DIRECT_PAIRS], F32)
@@ -289,46 +304,49 @@ def tile_evidentialhead_pb_kernel(tc, h_act, W3_words, W3_scales, b3, out_0, out
                 )
                 column += above
 
-        def pair_sums_group(g):
-            s_sorted = sorted_s[g]
-            shifted_belief = pair_pool.tile([P, GROUP, CLASSES], F32)
+        def pair_sums_group(n):
+            count = PAIR_GROUPS[n][1]
+            s_sorted = sorted_s[n]
+            shifted_belief = pair_pool.tile([P, count, CLASSES], F32)
             nc.scalar.activation(out=shifted_belief[:], in_=s_sorted[:], func=ACT.Exp, scale=2.0)
-            neg_tanh_sum = pair_pool.tile([P, GROUP, CLASSES], F32)
+            neg_tanh_sum = pair_pool.tile([P, count, CLASSES], F32)
             direct_sums(s_sorted, neg_tanh_sum, 0)
-            nc.scalar.activation(out=tip_tiles[g][:], in_=tip_tiles[g][:], func=ACT.Tanh)
-            for t in range(1, GROUP):
+            nc.scalar.activation(out=tip_tiles[n][:], in_=tip_tiles[n][:], func=ACT.Tanh)
+            for t in range(1, count):
                 direct_sums(s_sorted, neg_tanh_sum, t)
-            pair_results[g] = (shifted_belief, neg_tanh_sum)
+            pair_results[n] = (shifted_belief, neg_tanh_sum)
 
-        def tip_sums(g):
-            neg_tanh_sum = pair_results[g][1]
-            nc.vector.memset(neg_tanh_sum[:, :, DIRECT:CLASSES], 0.0)
-            level_sums = pair_pool.tile([P, TIP_BITS, GROUP * TIP // 2], F32)
-            for level, (half, blocks, part) in enumerate(tip_levels(tip_tiles[g])):
+        def tip_sums(n):
+            count = PAIR_GROUPS[n][1]
+            neg_tanh_sum = pair_results[n][1]
+            rectangles, squares = tip_parts(tip_tiles[n], count)
+            square_sums = pair_pool.tile([P, STEP_BITS, count * TIP // 2], F32)
+            for level, (half, piece) in enumerate(squares):
                 nc.vector.tensor_reduce(
-                    out=level_sums[:, level, :], in_=part.rearrange("p t b i j -> p (t b i) j"), axis=AXIS_X, op=ALU.add
+                    out=square_sums[:, level, :], in_=piece.rearrange("p t b i j -> p (t b i) j"), axis=AXIS_X, op=ALU.add
                 )
-            for level, (half, blocks, part) in enumerate(tip_levels(tip_tiles[g])):
-                lower = neg_tanh_sum[:, :, DIRECT:CLASSES].rearrange("p t (b s i) -> p t b s i", b=blocks, s=2)[:, :, :, 0, :]
+            nc.vector.memset(neg_tanh_sum[:, :, CLASSES - STEP : CLASSES], 0.0)
+            for classes_i, classes_j, piece in rectangles:
+                nc.vector.tensor_reduce(out=neg_tanh_sum[:, :, classes_i], in_=piece, axis=AXIS_X, op=ALU.add)
+            for level, (half, piece) in enumerate(squares):
+                lower = neg_tanh_sum[:, :, DIRECT:CLASSES].rearrange("p t (b s i) -> p t b s i", s=2, i=half)[:, :, :, 0, :]
                 nc.vector.tensor_tensor(
-                    out=lower,
-                    in0=lower,
-                    in1=level_sums[:, level, :].rearrange("p (t b i) -> p t b i", t=GROUP, b=blocks),
-                    op=ALU.add,
+                    out=lower, in0=lower, in1=square_sums[:, level, :].rearrange("p (t b i) -> p t b i", t=count, i=half), op=ALU.add
                 )
 
-        def dissonance_group(g):
-            shifted_belief, neg_tanh_sum = pair_results[g]
-            count_term = out_pool.tile([P, GROUP, CLASSES], F32)
+        def dissonance_group(n):
+            first, count = PAIR_GROUPS[n]
+            shifted_belief, neg_tanh_sum = pair_results[n]
+            count_term = out_pool.tile([P, count, CLASSES], F32)
             nc.vector.scalar_tensor_tensor(
                 out=count_term[:],
                 in0=shifted_belief[:],
                 scalar=-EPS / 2,
-                in1=classes_above[:].unsqueeze(1).to_broadcast([P, GROUP, CLASSES]),
+                in1=classes_above[:].unsqueeze(1).to_broadcast([P, count, CLASSES]),
                 op0=ALU.add,
                 op1=ALU.mult,
             )
-            tanh_term = out_pool.tile([P, GROUP, CLASSES], F32)
+            tanh_term = out_pool.tile([P, count, CLASSES], F32)
             nc.vector.scalar_tensor_tensor(
                 out=tanh_term[:], in0=shifted_belief[:], scalar=EPS / 2, in1=neg_tanh_sum[:], op0=ALU.add, op1=ALU.mult
             )
@@ -336,15 +354,15 @@ def tile_evidentialhead_pb_kernel(tc, h_act, W3_words, W3_scales, b3, out_0, out
             nc.vector.scalar_tensor_tensor(
                 out=tanh_term[:], in0=shifted_belief[:], scalar=-EPS / 2, in1=count_term[:], op0=ALU.add, op1=ALU.mult
             )
-            nc.vector.tensor_reduce(out=dissonance[:, group_tiles(g)], in_=tanh_term[:], axis=AXIS_X, op=ALU.add)
+            nc.vector.tensor_reduce(out=dissonance[:, first : first + count], in_=tanh_term[:], axis=AXIS_X, op=ALU.add)
 
         sort_group(0)
         tip_differences(0)
-        for g in range(GROUPS):
-            pair_sums_group(g)
-            if g + 1 < GROUPS:
-                sort_group(g + 1)
-                tip_differences(g + 1)
-            tip_sums(g)
-            dissonance_group(g)
+        for n in range(len(PAIR_GROUPS)):
+            pair_sums_group(n)
+            if n + 1 < len(PAIR_GROUPS):
+                sort_group(n + 1)
+                tip_differences(n + 1)
+            tip_sums(n)
+            dissonance_group(n)
         nc.sync.dma_start(out=dissonance_out, in_=dissonance[:])

from contextlib import ExitStack

import concourse.mybir as mybir
from concourse.masks import make_identity

F32 = mybir.dt.float32
BF16 = mybir.dt.bfloat16
I32 = mybir.dt.int32
U32 = mybir.dt.uint32
U8 = mybir.dt.uint8
FP8X4 = mybir.dt.float8_e4m3fn_x4
FP4X4 = mybir.dt.float4_e2m1fn_x4
ALU = mybir.AluOpType
ACT = mybir.ActivationFunctionType
AXIS_X = mybir.AxisListType.X

P = 128
ROWS = 5120
K = 1024
CLASSES = 128
CLASS_BITS = 7
EPS = 1e-8
PASSES = K // 512
TILES = ROWS // P
GROUP = 4
GROUPS = TILES // GROUP
STEP = 8
STEP_BITS = 3
TIP = 72
DIRECT = CLASSES - TIP
DIRECT_PAIRS = DIRECT * (CLASSES - 1) - DIRECT * (DIRECT - 1) // 2
TIP_PAIRS = TIP * (TIP - 1) // 2
PAIR_GROUPS = [(0, GROUP // 2), (GROUP // 2, GROUP // 2)] + [(first, GROUP) for first in range(GROUP, TILES, GROUP)]

FLOPS = 2 * ROWS * K * CLASSES


def compare_exchange_stage(nc, src, dst, width, dist):
    if dist == CLASSES // 2:
        parts, run = 1, CLASSES
    else:
        parts, run = 2, min(width, CLASSES // 2)
    pattern = "p (a d b s j) g -> p a d b s (j g)"
    sizes = dict(a=CLASSES // (run * parts), d=parts, b=run // (2 * dist), s=2, j=dist)
    src_view = src.rearrange(pattern, **sizes)
    dst_view = dst.rearrange(pattern, **sizes)
    for d in range(parts):
        falling = width < CLASSES and d == 1
        low_op, high_op = (ALU.max, ALU.min) if falling else (ALU.min, ALU.max)
        low = src_view[:, :, d, :, 0, :]
        high = src_view[:, :, d, :, 1, :]
        nc.vector.tensor_tensor(out=dst_view[:, :, d, :, 0, :], in0=low, in1=high, op=low_op)
        nc.vector.tensor_tensor(out=dst_view[:, :, d, :, 1, :], in0=low, in1=high, op=high_op)


def tip_parts(differences, count):
    rectangles = []
    squares = []
    start = 0
    for first in range(DIRECT, CLASSES - STEP, STEP):
        above = CLASSES - first - STEP
        size = count * STEP * above
        piece = differences[:, start : start + size].rearrange("p (t i j) -> p t i j", t=count, i=STEP)
        rectangles.append((slice(first, first + STEP), slice(first + STEP, CLASSES), piece))
        start += size
    for level in range(1, STEP_BITS + 1):
        half = STEP // 2**level
        size = count * (TIP // 2) * half
        piece = differences[:, start : start + size].rearrange("p (t b i j) -> p t b i j", t=count, i=half, j=half)
        squares.append((half, piece))
        start += size
    return rectangles, squares


def tile_evidentialhead_pb_kernel(tc, h_act, W3_words, W3_scales, b3, out_0, out_1, out_2, out_3, out_4):
    nc = tc.nc
    h_rows = h_act.rearrange("(p t) k -> p t k", t=TILES)
    alpha_out = out_0.rearrange("(p t) c -> p t c", t=TILES)
    evidence_out = out_1.rearrange("(p t) c -> p t c", t=TILES)
    prob_out = out_2.rearrange("(p t) c -> p t c", t=TILES)
    vacuity_out = out_3.rearrange("(p t) -> p t", t=TILES)
    dissonance_out = out_4.rearrange("(p t) -> p t", t=TILES)

    def group_tiles(g):
        return slice(g * GROUP, (g + 1) * GROUP)

    with ExitStack() as ctx:
        ctx.enter_context(tc.manual_schedule())
        const = ctx.enter_context(tc.tile_pool(name="const", bufs=1))
        whole = ctx.enter_context(tc.tile_pool(name="whole", bufs=1))

        work = whole.tile([P, TILES, CLASSES], F32)
        evidence = whole.tile([P, TILES, CLASSES], F32)
        alpha_sum = whole.tile([P, TILES], F32)
        inv_sum = whole.tile([P, TILES], F32)
        vacuity = whole.tile([P, TILES], F32)
        dissonance = whole.tile([P, TILES], F32)

        out_pool = ctx.enter_context(tc.tile_pool(name="outs", bufs=2))
        sort_pool = ctx.enter_context(tc.tile_pool(name="sort", bufs=1))
        pair_pool = ctx.enter_context(tc.tile_pool(name="pair", bufs=2))

        with ExitStack() as head:
            h_pool = head.enter_context(tc.tile_pool(name="h", bufs=3))
            mx_pool = head.enter_context(tc.tile_pool(name="mx", bufs=2))
            logit_pool = head.enter_context(tc.tile_pool(name="logit", bufs=1))
            psum_t = head.enter_context(tc.psum_pool(name="psum_t", bufs=6))
            psum_l = head.enter_context(tc.psum_pool(name="psum_l", bufs=2))

            h_tiles = {}

            def load_h(g):
                h_sb = h_pool.tile([P, GROUP, K], BF16, name="h_sb")
                nc.sync.dma_start(out=h_sb[:], in_=h_rows[:, group_tiles(g), :])
                h_tiles[g] = h_sb

            load_h(0)
            w_scales = const.tile([P, PASSES, CLASSES], U8, align_bytes=64)
            nc.vector.memset(w_scales[:].bitcast(I32), 0)
            w_words = const.tile([P, PASSES, 2 * CLASSES], U8, align_bytes=64)
            for c in range(PASSES):
                nc.sync.dma_start(out=w_words[:, c, :].bitcast(I32), in_=W3_words[c].bitcast(I32))
                for quadrant in range(4):
                    nc.sync.dma_start(
                        out=w_scales[32 * quadrant : 32 * quadrant + 4, c, :].bitcast(I32),
                        in_=W3_scales[c, 4 * quadrant : 4 * quadrant + 4, :].bitcast(I32),
                    )
            bias_rows = const.tile([P, CLASSES], BF16)
            nc.sync.dma_start(out=bias_rows[:], in_=b3.partition_broadcast(P))
            load_h(1)

            identity = const.tile([P, P], F32)
            make_identity(nc, identity[:])
            class_index = const.tile([P, CLASSES], I32)
            nc.gpsimd.iota(class_index[:], pattern=[[1, CLASSES]], base=0, channel_multiplier=0)
            classes_above = const.tile([P, CLASSES], F32)
            nc.vector.tensor_scalar(
                out=classes_above[:], in0=class_index[:], scalar1=-1.0, scalar2=float(CLASSES - 1), op0=ALU.mult, op1=ALU.add
            )
            one = const.tile([P, 1], F32)
            nc.vector.memset(one[:], 1.0)
            half_eps = const.tile([P, 1], F32)
            nc.vector.memset(half_eps[:], EPS / 2)

            logits = logit_pool.tile([P, TILES, CLASSES], F32)
            alpha = logit_pool.tile([P, TILES, CLASSES], F32)
            prob = logit_pool.tile([P, TILES, CLASSES], F32)

            grouped_tiles = {}
            mx_operands = {}

            def flip_group(g):
                h_sb = h_tiles[g]
                grouped = mx_pool.tile([P, GROUP, K], BF16, align_bytes=64)
                for t in range(GROUP):
                    h_words = h_sb[:, t, :].bitcast(F32)
                    flipped = psum_t.tile([P, PASSES, 2, P], F32)
                    for c in range(PASSES):
                        for u in range(2):
                            nc.tensor.transpose(flipped[:, c, u, :], h_words[:, 256 * c + u : 256 * (c + 1) : 2], identity[:])
                    copy_out = nc.vector.tensor_copy if t == GROUP - 1 else nc.scalar.copy
                    copy_out(
                        out=grouped[:, t, :].bitcast(F32).rearrange("p (c r u) -> p c r u", c=PASSES, u=2),
                        in_=flipped[:].rearrange("p c u r -> p c r u"),
                    )
                grouped_tiles[g] = grouped

            def quantise_group(g):
                codes = mx_pool.tile([P, GROUP, PASSES * P], U32, align_bytes=64)
                scales = mx_pool.tile([P, GROUP, PASSES * P], U8, align_bytes=64)
                nc.vector.quantize_mx(
                    out=codes[:].rearrange("p t w -> p (t w)").bitcast(FP8X4),
                    scales=scales[:].rearrange("p t w -> p (t w)"),
                    in_=grouped_tiles[g][:].rearrange("p t k -> p (t k)"),
                )
                mx_operands[g] = (codes, scales)

            def logits_group(g):
                codes, scales = mx_operands[g]
                acc = psum_l.tile([P, GROUP, CLASSES], F32)
                for t in range(GROUP):
                    for c in range(PASSES):
                        rows = slice(c * P, (c + 1) * P)
                        nc.tensor.matmul_mx(
                            out=acc[:, t, :],
                            lhsT=codes[:, t, rows].bitcast(FP8X4),
                            lhsT_scale=scales[:, t, rows],
                            rhs=w_words[:, c, :].bitcast(FP4X4),
                            rhs_scale=w_scales[:, c, :],
                            start=(c == 0),
                            stop=(c == PASSES - 1),
                        )
                tiles = group_tiles(g)
                nc.vector.tensor_tensor(
                    out=logits[:, tiles, :],
                    in0=acc[:],
                    in1=bias_rows[:].unsqueeze(1).to_broadcast([P, GROUP, CLASSES]),
                    op=ALU.add,
                )
                nc.vector.scalar_tensor_tensor(
                    out=work[:, tiles, :], in0=logits[:, tiles, :], scalar=-1.0, in1=logits[:, tiles, :], op0=ALU.mult, op1=ALU.min
                )

            def exp_group(g):
                tiles = group_tiles(g)
                nc.scalar.activation(out=work[:, tiles, :], in_=work[:, tiles, :], func=ACT.Exp)

            for g in range(GROUPS + 2):
                if g + 2 < GROUPS:
                    load_h(g + 2)
                if g < GROUPS:
                    flip_group(g)
                if 1 <= g <= GROUPS:
                    logits_group(g - 1)
                if g < GROUPS:
                    quantise_group(g)
                if g >= 2:
                    exp_group(g - 2)

            for g in range(GROUPS):
                tiles = group_tiles(g)
                nc.scalar.activation(out=work[:, tiles, :], in_=work[:, tiles, :], func=ACT.Ln, bias=one[:], scale=1.0)
                nc.vector.scalar_tensor_tensor(
                    out=evidence[:, tiles, :], in0=logits[:, tiles, :], scalar=0.0, in1=work[:, tiles, :], op0=ALU.max, op1=ALU.add
                )
                nc.sync.dma_start(out=evidence_out[:, tiles, :], in_=evidence[:, tiles, :])
            for g in range(GROUPS):
                for t in range(g * GROUP, (g + 1) * GROUP):
                    nc.scalar.activation(
                        out=alpha[:, t, :], in_=evidence[:, t, :], func=ACT.Identity, bias=one[:], scale=1.0, accum_out=alpha_sum[:, t : t + 1]
                    )
                nc.sync.dma_start(out=alpha_out[:, group_tiles(g), :], in_=alpha[:, group_tiles(g), :])
            nc.vector.reciprocal(out=inv_sum[:], in_=alpha_sum[:])
            nc.vector.tensor_scalar(out=vacuity[:], in0=inv_sum[:], scalar1=float(CLASSES), scalar2=None, op0=ALU.mult)
            nc.sync.dma_start(out=vacuity_out, in_=vacuity[:])
            for t in range(TILES):
                nc.scalar.activation(
                    out=work[:, t, :], in_=evidence[:, t, :], func=ACT.Ln, bias=half_eps[:], scale=inv_sum[:, t : t + 1]
                )
            for g in range(GROUPS):
                for t in range(g * GROUP, (g + 1) * GROUP):
                    nc.scalar.activation(
                        out=prob[:, t, :], in_=evidence[:, t, :], func=ACT.Identity, bias=inv_sum[:, t : t + 1], scale=inv_sum[:, t : t + 1]
                    )
                nc.sync.dma_start(out=prob_out[:, group_tiles(g), :], in_=prob[:, group_tiles(g), :])

        large_pool = ctx.enter_context(tc.tile_pool(name="large", bufs=2))

        sorted_s = {}
        tip_tiles = {}
        pair_results = {}

        def sort_group(n):
            first, count = PAIR_GROUPS[n]
            ping = sort_pool.tile([P, CLASSES, count], F32)
            pong = sort_pool.tile([P, CLASSES, count], F32)
            nc.vector.tensor_scalar(
                out=ping[:], in0=work[:, first : first + count, :].rearrange("p t c -> p c t"), scalar1=0.5, scalar2=None, op0=ALU.mult
            )
            src, dst = ping, pong
            for width_log in range(1, CLASS_BITS + 1):
                for dist_log in reversed(range(width_log)):
                    compare_exchange_stage(nc, src[:], dst[:], 2**width_log, 2**dist_log)
                    src, dst = dst, src
            s_sorted = pair_pool.tile([P, count, CLASSES], F32)
            nc.vector.tensor_copy(out=s_sorted[:], in_=src[:].rearrange("p c t -> p t c"))
            sorted_s[n] = s_sorted

        def tip_differences(n):
            count = PAIR_GROUPS[n][1]
            s_sorted = sorted_s[n]
            differences = large_pool.tile([P, count * TIP_PAIRS], F32)
            rectangles, squares = tip_parts(differences, count)
            for classes_i, classes_j, piece in rectangles:
                nc.vector.tensor_tensor(
                    out=piece,
                    in0=s_sorted[:, :, classes_i].unsqueeze(3).to_broadcast(piece.shape),
                    in1=s_sorted[:, :, classes_j].unsqueeze(2).to_broadcast(piece.shape),
                    op=ALU.subtract,
                )
            for half, piece in squares:
                halves = s_sorted[:, :, DIRECT:CLASSES].rearrange("p t (b s i) -> p t b s i", s=2, i=half)
                for i in range(half):
                    nc.vector.tensor_tensor(
                        out=piece[:, :, :, i, :],
                        in0=halves[:, :, :, 0, i : i + 1].to_broadcast(piece[:, :, :, i, :].shape),
                        in1=halves[:, :, :, 1, :],
                        op=ALU.subtract,
                    )
            tip_tiles[n] = differences

        def direct_sums(s_sorted, neg_tanh_sum, t):
            unread = large_pool.tile([P, DIRECT_PAIRS], F32)
            column = 0
            for i in range(DIRECT):
                above = CLASSES - 1 - i
                nc.scalar.activation(
                    out=unread[:, column : column + above],
                    in_=s_sorted[:, t, i + 1 : CLASSES],
                    func=ACT.Tanh,
                    bias=s_sorted[:, t, i : i + 1],
                    scale=-1.0,
                    accum_out=neg_tanh_sum[:, t, i : i + 1],
                )
                column += above

        def pair_sums_group(n):
            count = PAIR_GROUPS[n][1]
            s_sorted = sorted_s[n]
            shifted_belief = pair_pool.tile([P, count, CLASSES], F32)
            nc.scalar.activation(out=shifted_belief[:], in_=s_sorted[:], func=ACT.Exp, scale=2.0)
            neg_tanh_sum = pair_pool.tile([P, count, CLASSES], F32)
            direct_sums(s_sorted, neg_tanh_sum, 0)
            nc.scalar.activation(out=tip_tiles[n][:], in_=tip_tiles[n][:], func=ACT.Tanh)
            for t in range(1, count):
                direct_sums(s_sorted, neg_tanh_sum, t)
            pair_results[n] = (shifted_belief, neg_tanh_sum)

        def tip_sums(n):
            count = PAIR_GROUPS[n][1]
            neg_tanh_sum = pair_results[n][1]
            rectangles, squares = tip_parts(tip_tiles[n], count)
            square_sums = pair_pool.tile([P, STEP_BITS, count * TIP // 2], F32)
            for level, (half, piece) in enumerate(squares):
                nc.vector.tensor_reduce(
                    out=square_sums[:, level, :], in_=piece.rearrange("p t b i j -> p (t b i) j"), axis=AXIS_X, op=ALU.add
                )
            nc.vector.memset(neg_tanh_sum[:, :, CLASSES - STEP : CLASSES], 0.0)
            for classes_i, classes_j, piece in rectangles:
                nc.vector.tensor_reduce(out=neg_tanh_sum[:, :, classes_i], in_=piece, axis=AXIS_X, op=ALU.add)
            for level, (half, piece) in enumerate(squares):
                lower = neg_tanh_sum[:, :, DIRECT:CLASSES].rearrange("p t (b s i) -> p t b s i", s=2, i=half)[:, :, :, 0, :]
                nc.vector.tensor_tensor(
                    out=lower, in0=lower, in1=square_sums[:, level, :].rearrange("p (t b i) -> p t b i", t=count, i=half), op=ALU.add
                )

        def dissonance_group(n):
            first, count = PAIR_GROUPS[n]
            shifted_belief, neg_tanh_sum = pair_results[n]
            count_term = out_pool.tile([P, count, CLASSES], F32)
            nc.vector.scalar_tensor_tensor(
                out=count_term[:],
                in0=shifted_belief[:],
                scalar=-EPS / 2,
                in1=classes_above[:].unsqueeze(1).to_broadcast([P, count, CLASSES]),
                op0=ALU.add,
                op1=ALU.mult,
            )
            tanh_term = out_pool.tile([P, count, CLASSES], F32)
            nc.vector.scalar_tensor_tensor(
                out=tanh_term[:], in0=shifted_belief[:], scalar=EPS / 2, in1=neg_tanh_sum[:], op0=ALU.add, op1=ALU.mult
            )
            nc.vector.tensor_tensor(out=count_term[:], in0=count_term[:], in1=tanh_term[:], op=ALU.subtract)
            nc.vector.scalar_tensor_tensor(
                out=tanh_term[:], in0=shifted_belief[:], scalar=-EPS / 2, in1=count_term[:], op0=ALU.add, op1=ALU.mult
            )
            nc.vector.tensor_reduce(out=dissonance[:, first : first + count], in_=tanh_term[:], axis=AXIS_X, op=ALU.add)

        sort_group(0)
        tip_differences(0)
        for n in range(len(PAIR_GROUPS)):
            pair_sums_group(n)
            if n + 1 < len(PAIR_GROUPS):
                sort_group(n + 1)
                tip_differences(n + 1)
            tip_sums(n)
            dissonance_group(n)
        nc.sync.dma_start(out=dissonance_out, in_=dissonance[:])
